import numpy as np
import ml_dtypes


def mxq(x, axis, fmt="e4m3"):
    dtype, down = {"e4m3": (ml_dtypes.float8_e4m3fn, 7), "e5m2": (ml_dtypes.float8_e5m2, 14)}[fmt]
    v = np.moveaxis(np.asarray(x, np.float32).astype(ml_dtypes.bfloat16).astype(np.float64), axis, -1)
    blocks = v.reshape(v.shape[:-1] + (-1, 32))
    amax = np.abs(blocks).max(-1, keepdims=True)
    byte = np.maximum(np.where(amax > 0, np.frexp(amax)[1] - 1 + 127, 0) - down, 1)
    scale = np.exp2(byte - 127.0)
    codes = (blocks / scale).astype(np.float32).astype(dtype).astype(np.float64)
    return np.moveaxis((codes * scale).reshape(v.shape), -1, axis)


WIDE = False


def mx_kscale(k):
    if not WIDE:
        return np.ones(k)
    levels = np.array([10, -10, 5, -5, 0])
    a = np.random.permutation(np.resize(levels, k // 512 * 4)).reshape(k // 512, 4)
    idx = np.arange(k)
    return np.exp2(a[idx // 512, idx % 128 // 32])


BF16 = ml_dtypes.bfloat16


def bf(x):
    return np.asarray(x, np.float32).astype(BF16)


def f64(x):
    return np.asarray(x).astype(np.float64)


B, C, HI, WI, KH, KW, SH, SW, F1, F2, F3 = 2, 16, 70, 70, 8, 8, 2, 2, 1024, 256, 64
K1 = C * KH * KW
HO = (HI - KH) // SH + 1
WO = (WI - KW) // SW + 1
L = HO * WO


def unfold(x):
    cols = [x[:, :, i:i + (HO - 1) * SH + 1:SH, j:j + (WO - 1) * SW + 1:SW] for i in range(KH) for j in range(KW)]
    return np.stack(cols, axis=2).reshape(B, K1, L)


def setup_inputs():
    sc = mx_kscale(K1)[::KH * KW]
    s = np.repeat(sc, KH * KW)
    t = mx_kscale(F1)
    return {"x": bf(np.random.standard_normal((B, C, HI, WI)) * sc[None, :, None, None]),
            "w1": bf(np.random.standard_normal((K1, F1)) / np.sqrt(K1) / s[:, None] * t),
            "b1": bf(np.random.standard_normal(F1) * 0.3 * t),
            "w2": bf(np.random.standard_normal((F1, F2)) * 1.4 / np.sqrt(F1) / t[:, None]),
            "b2": bf(np.random.standard_normal(F2) * 0.3)}


def reference(x, w1, b1, w2, b2):
    p = unfold(f64(x)).transpose(0, 2, 1)
    h1 = np.maximum((mxq(p, 2, "e4m3") @ mxq(f64(w1), 0, "e4m3")) + f64(b1), 0.0)
    return np.maximum((mxq(h1, 2, "e4m3") @ mxq(f64(w2), 0, "e4m3")) + f64(b2), 0.0)

@@ -1,0 +1,212 @@
+from contextlib import ExitStack
+
+import concourse.mybir as mybir
+
+F32 = mybir.dt.float32
+BF16 = mybir.dt.bfloat16
+U32 = mybir.dt.uint32
+U8 = mybir.dt.uint8
+I32 = mybir.dt.int32
+FP8X4 = mybir.dt.float8_e4m3fn_x4
+RELU = mybir.ActivationFunctionType.Relu
+ADD = mybir.AluOpType.add
+
+FLOPS = 2 * 2048 * 1024 * 1024 + 2 * 2048 * 1024 * 256
+
+P = 128
+PITCH = 80
+
+
+def tile_mlpconv2d_pa_kernel(tc, x, w1, b1, w2, b2, out):
+    nc = tc.nc
+    with ExitStack() as ctx:
+        keep = ctx.enter_context(tc.tile_pool(name="keep", bufs=1))
+        psum = ctx.enter_context(tc.psum_pool(name="psum", bufs=8))
+
+        xr = [keep.tile([P, 32 * PITCH], BF16, name="xr%d" % n, align_bytes=64) for n in range(2)]
+        grp = [keep.tile([P, 2176], BF16, name="grp%d" % t, align_bytes=64) for t in range(4)]
+        qc = [keep.tile([P, 544], U32, name="qc%d" % t, align_bytes=64) for t in range(4)]
+        qs = [keep.tile([P, 544], U8, name="qs%d" % t, align_bytes=64) for t in range(4)]
+        qs2 = [keep.tile([P, 512], U8, name="qsb%d" % t, align_bytes=64) for t in range(4)]
+        w1r = keep.tile([P, 2, 4, 1024], BF16, name="w1r", align_bytes=64)
+        w1g = keep.tile([P, 2, 1024, 4], BF16, name="w1g", align_bytes=64)
+        w1c = keep.tile([P, 2, 1024], U32, name="w1c", align_bytes=64)
+        w1s = keep.tile([P, 2, 1024], U8, name="w1s", align_bytes=64)
+        w2r = keep.tile([P, 8, 256], BF16, name="w2r", align_bytes=64)
+        w2g = keep.tile([P, 2, 256, 4], BF16, name="w2g", align_bytes=64)
+        w2c = keep.tile([P, 2, 256], U32, name="w2c", align_bytes=64)
+        w2s = keep.tile([P, 2, 256], U8, name="w2s", align_bytes=64)
+        b1r = keep.tile([P, 8], BF16, name="b1r")
+        b1f = keep.tile([P, 8], F32, name="b1f")
+        b2z = keep.tile([P, 256], BF16, name="b2z")
+        ones = keep.tile([P, P], BF16, name="ones")
+        b2bc = keep.tile([P, 256], F32, name="b2bc")
+        hpl = [keep.tile([P, 8, 512], BF16, name="hpl%d" % t, align_bytes=64) for t in range(4)]
+        hgr = [keep.tile([P, 2, 512, 4], BF16, name="hgr%d" % t, align_bytes=64) for t in range(4)]
+        hc = [keep.tile([P, 2, 512], U32, name="hc%d" % t, align_bytes=64) for t in range(4)]
+        hs = [keep.tile([P, 2, 512], U8, name="hs%d" % t, align_bytes=64) for t in range(4)]
+        res = [keep.tile([P, 4, 256], F32, name="res%d" % t) for t in range(4)]
+
+        xv = x.rearrange("n c (hh two) w -> n c hh two w", two=2)
+
+        def load_x(eng, n, u0, nu, i):
+            dst = xr[n][:].rearrange("p (u w) -> p u w", w=PITCH)
+            eng.dma_start(
+                out=dst[i:P:8, u0 : u0 + nu, 0:70],
+                in_=xv[n, :, u0 + i // 2 : u0 + i // 2 + nu, i % 2, :],
+            )
+
+        for t in range(4):
+            nc.vector.memset(qs[t][:].bitcast(I32), 0)
+        nc.vector.memset(b2z[:], 0.0)
+        nc.vector.memset(ones[:], 1.0)
+
+        for i in range(4):
+            load_x(nc.sync, 0, 0, 16, i)
+            load_x(nc.scalar, 0, 0, 16, i + 4)
+        with nc.allow_non_contiguous_dma(reason="bias, one element to a partition"):
+            nc.gpsimd.dma_start(out=b1r[:], in_=b1.rearrange("(t p) -> p t", p=P))
+        nc.gpsimd.dma_start(out=b2z[0:1, :], in_=b2.rearrange("(o n) -> o n", o=1))
+        w1v = w1.rearrange("(p jh t) f -> p jh t f", jh=2, t=4)
+        for jh in range(2):
+            nc.sync.dma_start(out=w1r[:, jh, :, :], in_=w1v[:, jh, :, :])
+        for i in range(8):
+            load_x(nc.sync, 0, 16, 16, i)
+        nc.sync.dma_start(out=w2r[:], in_=w2.rearrange("(gt p) n -> p gt n", p=P))
+        for i in range(8):
+            load_x(nc.sync, 1, 0, 32, i)
+
+        nc.vector.tensor_copy(out=b1f[:], in_=b1r[:])
+        b2ps = psum.tile([P, 512], F32, name="b2ps", tag="bank")
+        nc.tensor.matmul(out=b2ps[:, 0:256], lhsT=ones[:], rhs=b2z[:], start=True, stop=True)
+        nc.vector.tensor_copy(out=b2bc[:], in_=b2ps[:, 0:256])
+
+        def prep_p(t):
+            n, uh = t // 2, t % 2
+            x32 = xr[n][:].bitcast(F32).rearrange("p (u w) -> p u w", w=PITCH // 2)
+            g32 = grp[t][:].bitcast(F32).rearrange("p (a b u th) -> p a b u th", a=17, b=2, u=16)
+            for b in range(2):
+                nc.vector.tensor_copy(
+                    out=g32[:, :, b, :, :],
+                    in_=x32[:, 16 * uh : 16 * uh + 16, b : b + 34].rearrange("p u (a th) -> p a u th", th=2),
+                )
+            nc.vector.quantize_mx(out=qc[t][:, 0:512].bitcast(FP8X4), scales=qs[t][:, 0:512], in_=grp[t][:, 0:2048])
+            nc.vector.quantize_mx(
+                out=qc[t][:, 512:544].bitcast(FP8X4), scales=qs[t][:, 512:544], in_=grp[t][:, 2048:2176]
+            )
+            nc.vector.tensor_copy(out=qs2[t][:].bitcast(I32), in_=qs[t][:, 32:544].bitcast(I32))
+
+        def regroup(eng_copy, dst, src):
+            eng_copy(
+                out=dst.rearrange("p (c i) t -> p c t i", i=4),
+                in_=src.rearrange("p t (c i) -> p c t i", i=4),
+            )
+
+        def prep_w1(jh, pair):
+            f0 = 256 * pair
+            regroup(nc.vector.tensor_copy, w1g[:, jh, f0 : f0 + 128, :], w1r[:, jh, :, f0 : f0 + 128])
+            regroup(nc.scalar.copy, w1g[:, jh, f0 + 128 : f0 + 256, :], w1r[:, jh, :, f0 + 128 : f0 + 256])
+
+        def quant_w1(jh, pair):
+            f0 = 256 * pair
+            nc.vector.quantize_mx(
+                out=w1c[:, jh, f0 : f0 + 256].bitcast(FP8X4),
+                scales=w1s[:, jh, f0 : f0 + 256],
+                in_=w1g[:, jh, f0 : f0 + 256, :].rearrange("p f t -> p (f t)"),
+            )
+
+        def l1_pass(t, ft, jh, bank):
+            rs = qs[t][:, 0:512] if jh == 0 else qs2[t][:, 0:512]
+            nc.tensor.matmul_mx(
+                out=bank[:],
+                lhsT=w1c[:, jh, P * ft : P * ft + P].bitcast(FP8X4),
+                lhsT_scale=w1s[:, jh, P * ft : P * ft + P],
+                rhs=qc[t][:, 32 * jh : 32 * jh + 512].bitcast(FP8X4),
+                rhs_scale=rs,
+                start=(jh == 0),
+                stop=(jh == 1),
+            )
+
+        def evac(t, ft, bank):
+            nc.scalar.activation(
+                out=hpl[t][:, ft, :].rearrange("p (u a b) -> p u a b", a=16, b=2),
+                in_=bank[:].rearrange("p (a b u) -> p u a b", a=16, b=2),
+                func=RELU,
+                bias=b1f[:, ft : ft + 1],
+                scale=1.0,
+            )
+
+        def regroup_h(t, g):
+            regroup(nc.vector.tensor_copy, hgr[t][:, g, :, :], hpl[t][:, 4 * g : 4 * g + 4, :])
+
+        def quant_h(t, g):
+            nc.vector.quantize_mx(
+                out=hc[t][:, g, :].bitcast(FP8X4),
+                scales=hs[t][:, g, :],
+                in_=hgr[t][:, g, :, :].rearrange("p c t -> p (c t)"),
+            )
+
+        def l2(t, k):
+            n, uh = t // 2, t % 2
+            acc = psum.tile([P, 2, 256], F32, name="acc%d_%d" % (t, k), tag="bank")
+            for s in range(2):
+                c0 = P * (2 * k + s)
+                for g in range(2):
+                    nc.tensor.matmul_mx(
+                        out=acc[:, s, :],
+                        lhsT=hc[t][:, g, c0 : c0 + P].bitcast(FP8X4),
+                        lhsT_scale=hs[t][:, g, c0 : c0 + P],
+                        rhs=w2c[:, g, :].bitcast(FP8X4),
+                        rhs_scale=w2s[:, g, :],
+                        start=(g == 0),
+                        stop=(g == 1),
+                    )
+            r = res[t][:, 2 * k : 2 * k + 2, :]
+            nc.vector.tensor_tensor(out=r, in0=acc[:], in1=b2bc[:].unsqueeze(1).to_broadcast([P, 2, 256]), op=ADD)
+            nc.scalar.activation(out=r, in_=r, func=RELU)
+            r0 = 512 * uh + 256 * k
+            nc.sync.dma_start(out=out[n, r0 : r0 + 256, :].rearrange("(s p) f -> p s f", p=P), in_=r)
+
+        prep_p(0)
+        banks = {}
+        for ft in range(8):
+            banks[(0, ft)] = psum.tile([P, 512], F32, name="l1_0_%d" % ft, tag="bank")
+        for jh in range(2):
+            prep_w1(jh, 0)
+            for pair in range(4):
+                if pair < 3:
+                    prep_w1(jh, pair + 1)
+                quant_w1(jh, pair)
+                for ft in (2 * pair, 2 * pair + 1):
+                    l1_pass(0, ft, jh, banks[(0, ft)])
+        prep_p(1)
+        for g in range(2):
+            regroup(nc.vector.tensor_copy if g == 0 else nc.scalar.copy, w2g[:, g, :, :], w2r[:, 4 * g : 4 * g + 4, :])
+        nc.vector.quantize_mx(
+            out=w2c[:].rearrange("p g n -> p (g n)").bitcast(FP8X4),
+            scales=w2s[:].rearrange("p g n -> p (g n)"),
+            in_=w2g[:].rearrange("p g n t -> p (g n t)"),
+        )
+
+        LEAD = 6
+        for u in range(32):
+            t, ft = divmod(u, 8)
+            evac(t, ft, banks[(t, ft)])
+            if ft == 3:
+                regroup_h(t, 0)
+            if ft == 5:
+                quant_h(t, 0)
+            if ft == 7:
+                regroup_h(t, 1)
+                quant_h(t, 1)
+            nxt = u + LEAD
+            if 8 <= nxt < 32:
+                bank = psum.tile([P, 512], F32, name="l1_%d" % nxt, tag="bank")
+                banks[divmod(nxt, 8)] = bank
+                for jh in range(2):
+                    l1_pass(nxt // 8, nxt % 8, jh, bank)
+            if ft == 7:
+                for k in range(2):
+                    l2(t, k)
+            if u in (3, 11):
+                prep_p(u // 8 + 2)

@@ -28,15 +28,16 @@ def tile_mlpconv2d_pa_kernel(tc, x, w1, b1, w2, b2, out):
         qc = [keep.tile([P, 544], U32, name="qc%d" % t, align_bytes=64) for t in range(4)]
         qs = [keep.tile([P, 544], U8, name="qs%d" % t, align_bytes=64) for t in range(4)]
         qs2 = [keep.tile([P, 512], U8, name="qsb%d" % t, align_bytes=64) for t in range(4)]
-        w1r = keep.tile([P, 2, 4, 1024], BF16, name="w1r", align_bytes=64)
-        w1g = keep.tile([P, 2, 1024, 4], BF16, name="w1g", align_bytes=64)
-        w1c = keep.tile([P, 2, 1024], U32, name="w1c", align_bytes=64)
-        w1s = keep.tile([P, 2, 1024], U8, name="w1s", align_bytes=64)
+        w1r = keep.tile([P, 8, 1024], BF16, name="w1r", align_bytes=64)
+        w1g = keep.tile([P, 4, 2, 256, 4], BF16, name="w1g", align_bytes=64)
+        w1c = keep.tile([P, 4, 2, 256], U32, name="w1c", align_bytes=64)
+        w1s = keep.tile([P, 4, 2, 256], U8, name="w1s", align_bytes=64)
         w2r = keep.tile([P, 8, 256], BF16, name="w2r", align_bytes=64)
         w2g = keep.tile([P, 2, 256, 4], BF16, name="w2g", align_bytes=64)
         w2c = keep.tile([P, 2, 256], U32, name="w2c", align_bytes=64)
         w2s = keep.tile([P, 2, 256], U8, name="w2s", align_bytes=64)
-        b1r = keep.tile([P, 8], BF16, name="b1r")
+        b1r = keep.tile([P, 32], BF16, name="b1r", align_bytes=64)
+        b1t = keep.tile([P, 32], BF16, name="b1t", align_bytes=64)
         b1f = keep.tile([P, 8], F32, name="b1f")
         b2z = keep.tile([P, 256], BF16, name="b2z")
         ones = keep.tile([P, P], BF16, name="ones")
@@ -56,32 +57,30 @@ def tile_mlpconv2d_pa_kernel(tc, x, w1, b1, w2, b2, out):
                 in_=xv[n, :, u0 + i // 2 : u0 + i // 2 + nu, i % 2, :],
             )
 
-        for t in range(4):
-            nc.vector.memset(qs[t][:].bitcast(I32), 0)
+        ctx.enter_context(tc.manual_schedule())
+        nc.vector.memset(b1r[:], 0.0)
         nc.vector.memset(b2z[:], 0.0)
         nc.vector.memset(ones[:], 1.0)
-
+        for t in range(4):
+            nc.vector.memset(qs[t][:].bitcast(I32), 0)
         for i in range(4):
             load_x(nc.sync, 0, 0, 16, i)
             load_x(nc.scalar, 0, 0, 16, i + 4)
-        with nc.allow_non_contiguous_dma(reason="bias, one element to a partition"):
-            nc.gpsimd.dma_start(out=b1r[:], in_=b1.rearrange("(t p) -> p t", p=P))
-        nc.gpsimd.dma_start(out=b2z[0:1, :], in_=b2.rearrange("(o n) -> o n", o=1))
-        w1v = w1.rearrange("(p jh t) f -> p jh t f", jh=2, t=4)
-        for jh in range(2):
-            nc.sync.dma_start(out=w1r[:, jh, :, :], in_=w1v[:, jh, :, :])
-        for i in range(8):
-            load_x(nc.sync, 0, 16, 16, i)
+        b1v = b1.rearrange("(ft q c) -> q ft c", q=4, c=32)
+        for q in range(4):
+            nc.scalar.dma_start(out=b1r[32 * q : 32 * q + 8, :], in_=b1v[q])
+        nc.scalar.dma_start(out=b2z[0:1, :], in_=b2.rearrange("(o n) -> o n", o=1))
+        w1v = w1.rearrange("(p r) f -> p r f", r=8)
+        for j in range(4):
+            if j == 3:
+                for i in range(8):
+                    load_x(nc.sync, 0, 16, 16, i)
+            nc.sync.dma_start(out=w1r[:, :, 256 * j : 256 * j + 256], in_=w1v[:, :, 256 * j : 256 * j + 256])
         nc.sync.dma_start(out=w2r[:], in_=w2.rearrange("(gt p) n -> p gt n", p=P))
         for i in range(8):
             load_x(nc.sync, 1, 0, 32, i)
 
-        nc.vector.tensor_copy(out=b1f[:], in_=b1r[:])
-        b2ps = psum.tile([P, 512], F32, name="b2ps", tag="bank")
-        nc.tensor.matmul(out=b2ps[:, 0:256], lhsT=ones[:], rhs=b2z[:], start=True, stop=True)
-        nc.vector.tensor_copy(out=b2bc[:], in_=b2ps[:, 0:256])
-
-        def prep_p(t):
+        def copy_p(t):
             n, uh = t // 2, t % 2
             x32 = xr[n][:].bitcast(F32).rearrange("p (u w) -> p u w", w=PITCH // 2)
             g32 = grp[t][:].bitcast(F32).rearrange("p (a b u th) -> p a b u th", a=17, b=2, u=16)
@@ -90,6 +89,8 @@ def tile_mlpconv2d_pa_kernel(tc, x, w1, b1, w2, b2, out):
                     out=g32[:, :, b, :, :],
                     in_=x32[:, 16 * uh : 16 * uh + 16, b : b + 34].rearrange("p u (a th) -> p a u th", th=2),
                 )
+
+        def quant_p(t):
             nc.vector.quantize_mx(out=qc[t][:, 0:512].bitcast(FP8X4), scales=qs[t][:, 0:512], in_=grp[t][:, 0:2048])
             nc.vector.quantize_mx(
                 out=qc[t][:, 512:544].bitcast(FP8X4), scales=qs[t][:, 512:544], in_=grp[t][:, 2048:2176]
@@ -102,35 +103,41 @@ def tile_mlpconv2d_pa_kernel(tc, x, w1, b1, w2, b2, out):
                 in_=src.rearrange("p t (c i) -> p c t i", i=4),
             )
 
-        def prep_w1(jh, pair):
-            f0 = 256 * pair
-            regroup(nc.vector.tensor_copy, w1g[:, jh, f0 : f0 + 128, :], w1r[:, jh, :, f0 : f0 + 128])
-            regroup(nc.scalar.copy, w1g[:, jh, f0 + 128 : f0 + 256, :], w1r[:, jh, :, f0 + 128 : f0 + 256])
+        def regroup_w1(j):
+            cols = slice(256 * j, 256 * j + 256)
+            regroup(nc.vector.tensor_copy, w1g[:, j, 0, :, :], w1r[:, 0:4, cols])
+            regroup(nc.scalar.copy, w1g[:, j, 1, :, :], w1r[:, 4:8, cols])
 
-        def quant_w1(jh, pair):
-            f0 = 256 * pair
+        def quant_w1(j):
             nc.vector.quantize_mx(
-                out=w1c[:, jh, f0 : f0 + 256].bitcast(FP8X4),
-                scales=w1s[:, jh, f0 : f0 + 256],
-                in_=w1g[:, jh, f0 : f0 + 256, :].rearrange("p f t -> p (f t)"),
+                out=w1c[:, j, :, :].rearrange("p h f -> p (h f)").bitcast(FP8X4),
+                scales=w1s[:, j, :, :].rearrange("p h f -> p (h f)"),
+                in_=w1g[:, j, :, :, :].rearrange("p h f t -> p (h f t)"),
             )
 
-        def l1_pass(t, ft, jh, bank):
-            rs = qs[t][:, 0:512] if jh == 0 else qs2[t][:, 0:512]
-            nc.tensor.matmul_mx(
-                out=bank[:],
-                lhsT=w1c[:, jh, P * ft : P * ft + P].bitcast(FP8X4),
-                lhsT_scale=w1s[:, jh, P * ft : P * ft + P],
-                rhs=qc[t][:, 32 * jh : 32 * jh + 512].bitcast(FP8X4),
-                rhs_scale=rs,
-                start=(jh == 0),
-                stop=(jh == 1),
-            )
+        banks = {}
 
-        def evac(t, ft, bank):
+        def l1(u):
+            t, ft = divmod(u, 8)
+            bank = psum.tile([P, 512], F32, name="l1_%d" % u, tag="bank")
+            banks[u] = bank
+            j, c0 = ft // 2, P * (ft % 2)
+            for jh in range(2):
+                nc.tensor.matmul_mx(
+                    out=bank[:],
+                    lhsT=w1c[:, j, jh, c0 : c0 + P].bitcast(FP8X4),
+                    lhsT_scale=w1s[:, j, jh, c0 : c0 + P],
+                    rhs=qc[t][:, 32 * jh : 32 * jh + 512].bitcast(FP8X4),
+                    rhs_scale=qs[t][:, 0:512] if jh == 0 else qs2[t][:, 0:512],
+                    start=(jh == 0),
+                    stop=(jh == 1),
+                )
+
+        def evac(u):
+            t, ft = divmod(u, 8)
             nc.scalar.activation(
                 out=hpl[t][:, ft, :].rearrange("p (u a b) -> p u a b", a=16, b=2),
-                in_=bank[:].rearrange("p (a b u) -> p u a b", a=16, b=2),
+                in_=banks[u][:].rearrange("p (a b u) -> p u a b", a=16, b=2),
                 func=RELU,
                 bias=b1f[:, ft : ft + 1],
                 scale=1.0,
@@ -146,9 +153,11 @@ def tile_mlpconv2d_pa_kernel(tc, x, w1, b1, w2, b2, out):
                 in_=hgr[t][:, g, :, :].rearrange("p c t -> p (c t)"),
             )
 
+        accs = {}
+
         def l2(t, k):
-            n, uh = t // 2, t % 2
             acc = psum.tile([P, 2, 256], F32, name="acc%d_%d" % (t, k), tag="bank")
+            accs[(t, k)] = acc
             for s in range(2):
                 c0 = P * (2 * k + s)
                 for g in range(2):
@@ -161,52 +170,82 @@ def tile_mlpconv2d_pa_kernel(tc, x, w1, b1, w2, b2, out):
                         start=(g == 0),
                         stop=(g == 1),
                     )
+
+        def add_b2(t, k):
+            nc.vector.tensor_tensor(
+                out=res[t][:, 2 * k : 2 * k + 2, :],
+                in0=accs[(t, k)][:],
+                in1=b2bc[:].unsqueeze(1).to_broadcast([P, 2, 256]),
+                op=ADD,
+            )
+
+        def relu_store(t, k):
+            n, uh = t // 2, t % 2
             r = res[t][:, 2 * k : 2 * k + 2, :]
-            nc.vector.tensor_tensor(out=r, in0=acc[:], in1=b2bc[:].unsqueeze(1).to_broadcast([P, 2, 256]), op=ADD)
             nc.scalar.activation(out=r, in_=r, func=RELU)
             r0 = 512 * uh + 256 * k
             nc.sync.dma_start(out=out[n, r0 : r0 + 256, :].rearrange("(s p) f -> p s f", p=P), in_=r)
 
-        prep_p(0)
-        banks = {}
-        for ft in range(8):
-            banks[(0, ft)] = psum.tile([P, 512], F32, name="l1_0_%d" % ft, tag="bank")
-        for jh in range(2):
-            prep_w1(jh, 0)
-            for pair in range(4):
-                if pair < 3:
-                    prep_w1(jh, pair + 1)
-                quant_w1(jh, pair)
-                for ft in (2 * pair, 2 * pair + 1):
-                    l1_pass(0, ft, jh, banks[(0, ft)])
-        prep_p(1)
+        LEAD = 6
+
+        b2ps = psum.tile([P, 512], F32, name="b2ps", tag="bank")
+        nc.tensor.matmul(out=b2ps[:, 0:256], lhsT=ones[:], rhs=b2z[:], start=True, stop=True)
+        copy_p(0)
+        regroup_w1(0)
+        quant_p(0)
+        nc.vector.transpose(out=b1t[:], in_=b1r[:])
+        nc.vector.tensor_copy(out=b1f[:], in_=b1t[:, 0:8])
+        for j in range(4):
+            quant_w1(j)
+            l1(2 * j)
+            l1(2 * j + 1)
+            if j < 3:
+                regroup_w1(j + 1)
+            evac(2 * j)
+            evac(2 * j + 1)
+            if j == 0:
+                nc.vector.tensor_copy(out=b2bc[:], in_=b2ps[:, 0:256])
+            if j == 2:
+                copy_p(1)
+                regroup_h(0, 0)
+        quant_p(1)
         for g in range(2):
-            regroup(nc.vector.tensor_copy if g == 0 else nc.scalar.copy, w2g[:, g, :, :], w2r[:, 4 * g : 4 * g + 4, :])
+            regroup(nc.vector.tensor_copy, w2g[:, g, :, :], w2r[:, 4 * g : 4 * g + 4, :])
+        quant_h(0, 0)
         nc.vector.quantize_mx(
             out=w2c[:].rearrange("p g n -> p (g n)").bitcast(FP8X4),
             scales=w2s[:].rearrange("p g n -> p (g n)"),
             in_=w2g[:].rearrange("p g n t -> p (g n t)"),
         )
+        for u in range(8, 8 + LEAD):
+            l1(u)
 
-        LEAD = 6
-        for u in range(32):
-            t, ft = divmod(u, 8)
-            evac(t, ft, banks[(t, ft)])
-            if ft == 3:
+        for t in range(1, 5):
+            def step(ft):
+                if t < 4:
+                    evac(8 * t + ft)
+                    if 8 * t + ft + LEAD < 32:
+                        l1(8 * t + ft + LEAD)
+
+            step(0)
+            regroup_h(t - 1, 1)
+            if t + 1 < 4:
+                copy_p(t + 1)
+            step(1)
+            quant_h(t - 1, 1)
+            l2(t - 1, 0)
+            l2(t - 1, 1)
+            if t + 1 < 4:
+                quant_p(t + 1)
+            step(2)
+            add_b2(t - 1, 0)
+            step(3)
+            if t < 4:
                 regroup_h(t, 0)
-            if ft == 5:
+            add_b2(t - 1, 1)
+            if t < 4:
                 quant_h(t, 0)
-            if ft == 7:
-                regroup_h(t, 1)
-                quant_h(t, 1)
-            nxt = u + LEAD
-            if 8 <= nxt < 32:
-                bank = psum.tile([P, 512], F32, name="l1_%d" % nxt, tag="bank")
-                banks[divmod(nxt, 8)] = bank
-                for jh in range(2):
-                    l1_pass(nxt // 8, nxt % 8, jh, bank)
-            if ft == 7:
-                for k in range(2):
-                    l2(t, k)
-            if u in (3, 11):
-                prep_p(u // 8 + 2)
+            for ft in range(4, 8):
+                step(ft)
+            relu_store(t - 1, 0)
+            relu_store(t - 1, 1)

@@ -14,7 +14,7 @@ ADD = mybir.AluOpType.add
 FLOPS = 2 * 2048 * 1024 * 1024 + 2 * 2048 * 1024 * 256
 
 P = 128
-PITCH = 80
+PITCH = 112
 
 
 def tile_mlpconv2d_pa_kernel(tc, x, w1, b1, w2, b2, out):
@@ -23,21 +23,21 @@ def tile_mlpconv2d_pa_kernel(tc, x, w1, b1, w2, b2, out):
         keep = ctx.enter_context(tc.tile_pool(name="keep", bufs=1))
         psum = ctx.enter_context(tc.psum_pool(name="psum", bufs=8))
 
-        xr = [keep.tile([P, 32 * PITCH], BF16, name="xr%d" % n, align_bytes=64) for n in range(2)]
-        grp = [keep.tile([P, 2176], BF16, name="grp%d" % t, align_bytes=64) for t in range(4)]
-        qc = [keep.tile([P, 544], U32, name="qc%d" % t, align_bytes=64) for t in range(4)]
-        qs = [keep.tile([P, 544], U8, name="qs%d" % t, align_bytes=64) for t in range(4)]
-        qs2 = [keep.tile([P, 512], U8, name="qsb%d" % t, align_bytes=64) for t in range(4)]
-        w1r = keep.tile([P, 8, 1024], BF16, name="w1r", align_bytes=64)
-        w1g = keep.tile([P, 4, 2, 256, 4], BF16, name="w1g", align_bytes=64)
-        w1c = keep.tile([P, 4, 2, 256], U32, name="w1c", align_bytes=64)
-        w1s = keep.tile([P, 4, 2, 256], U8, name="w1s", align_bytes=64)
+        xr0 = keep.tile([P, 32 * PITCH], BF16, name="xr0", align_bytes=64)
+        xr = [xr0]
+        grp = [keep.tile([P, 2304], BF16, name="grp%d" % t, align_bytes=64) for t in range(4)]
+        qc = [keep.tile([P, 576], U32, name="qc%d" % t, align_bytes=64) for t in range(4)]
+        qs = [keep.tile([P, 576], U8, name="qs%d" % t, align_bytes=64) for t in range(4)]
+        w1r = [keep.tile([P, 4, 1024], BF16, name="w1r%d" % jh, tag="raw%d" % jh, align_bytes=64) for jh in range(2)]
+        w1g = keep.tile([P, 2, 1024, 4], BF16, name="w1g", align_bytes=64)
+        w1c = keep.tile([P, 2, 1024], U32, name="w1c", align_bytes=64)
+        w1s = keep.tile([P, 2, 1024], U8, name="w1s", align_bytes=64)
         w2r = keep.tile([P, 8, 256], BF16, name="w2r", align_bytes=64)
         w2g = keep.tile([P, 2, 256, 4], BF16, name="w2g", align_bytes=64)
         w2c = keep.tile([P, 2, 256], U32, name="w2c", align_bytes=64)
         w2s = keep.tile([P, 2, 256], U8, name="w2s", align_bytes=64)
-        b1r = keep.tile([P, 32], BF16, name="b1r", align_bytes=64)
-        b1t = keep.tile([P, 32], BF16, name="b1t", align_bytes=64)
+        b1r = keep.tile([P, 256], BF16, name="b1r", align_bytes=64)
+        b1t = keep.tile([P, 256], BF16, name="b1t", align_bytes=64)
         b1f = keep.tile([P, 8], F32, name="b1f")
         b2z = keep.tile([P, 256], BF16, name="b2z")
         ones = keep.tile([P, P], BF16, name="ones")
@@ -50,8 +50,8 @@ def tile_mlpconv2d_pa_kernel(tc, x, w1, b1, w2, b2, out):
 
         xv = x.rearrange("n c (hh two) w -> n c hh two w", two=2)
 
-        def load_x(eng, n, u0, nu, i):
-            dst = xr[n][:].rearrange("p (u w) -> p u w", w=PITCH)
+        def load_x(eng, tile_, n, u0, nu, i):
+            dst = tile_[:].rearrange("p (u w) -> p u w", w=PITCH)
             eng.dma_start(
                 out=dst[i:P:8, u0 : u0 + nu, 0:70],
                 in_=xv[n, :, u0 + i // 2 : u0 + i // 2 + nu, i % 2, :],
@@ -61,41 +61,40 @@ def tile_mlpconv2d_pa_kernel(tc, x, w1, b1, w2, b2, out):
         nc.vector.memset(b1r[:], 0.0)
         nc.vector.memset(b2z[:], 0.0)
         nc.vector.memset(ones[:], 1.0)
-        for t in range(4):
-            nc.vector.memset(qs[t][:].bitcast(I32), 0)
-        for i in range(4):
-            load_x(nc.sync, 0, 0, 16, i)
-            load_x(nc.scalar, 0, 0, 16, i + 4)
-        b1v = b1.rearrange("(ft q c) -> q ft c", q=4, c=32)
-        for q in range(4):
-            nc.scalar.dma_start(out=b1r[32 * q : 32 * q + 8, :], in_=b1v[q])
-        nc.scalar.dma_start(out=b2z[0:1, :], in_=b2.rearrange("(o n) -> o n", o=1))
-        w1v = w1.rearrange("(p r) f -> p r f", r=8)
-        for j in range(4):
-            if j == 3:
-                for i in range(8):
-                    load_x(nc.sync, 0, 16, 16, i)
-            nc.sync.dma_start(out=w1r[:, :, 256 * j : 256 * j + 256], in_=w1v[:, :, 256 * j : 256 * j + 256])
-        nc.sync.dma_start(out=w2r[:], in_=w2.rearrange("(gt p) n -> p gt n", p=P))
+        w1v = w1.rearrange("(p jh t) f -> p jh t f", jh=2, t=4)
+        nc.gpsimd.dma_start(
+            out=b1r[0:P:32, :].rearrange("q (ft c) -> q ft c", c=32), in_=b1.rearrange("(ft q c) -> q ft c", q=4, c=32)
+        )
+        nc.gpsimd.dma_start(out=b2z[0:1, :], in_=b2.rearrange("(o n) -> o n", o=1))
+        for i in range(7):
+            load_x(nc.scalar if i < 4 else nc.sync, xr0, 0, 0, 16, i)
+        nc.sync.dma_start(out=w1r[0][:], in_=w1v[:, 0, :, :])
+        load_x(nc.sync, xr0, 0, 0, 16, 7)
+        nc.sync.dma_start(out=w1r[1][:], in_=w1v[:, 1, :, :])
         for i in range(8):
-            load_x(nc.sync, 1, 0, 32, i)
+            load_x(nc.sync, xr0, 0, 16, 16, i)
+        nc.sync.dma_start(out=w2r[:], in_=w2.rearrange("(gt p) n -> p gt n", p=P))
 
         def copy_p(t):
             n, uh = t // 2, t % 2
-            x32 = xr[n][:].bitcast(F32).rearrange("p (u w) -> p u w", w=PITCH // 2)
-            g32 = grp[t][:].bitcast(F32).rearrange("p (a b u th) -> p a b u th", a=17, b=2, u=16)
-            for b in range(2):
+            x32 = xr[n][:].bitcast(F32).rearrange("p (u w) -> p u w", w=PITCH // 2)[:, 16 * uh : 16 * uh + 16, :]
+            g32 = grp[t][:].bitcast(F32).rearrange("p (e o u vh th) -> p e o u vh th", e=9, o=2, u=16, vh=2)
+            for o in range(2):
                 nc.vector.tensor_copy(
-                    out=g32[:, :, b, :, :],
-                    in_=x32[:, 16 * uh : 16 * uh + 16, b : b + 34].rearrange("p u (a th) -> p a u th", th=2),
+                    out=g32[:, 0:8, o, :, :, :],
+                    in_=x32[:, :, o : o + 32].rearrange("p u (vh e th) -> p e u vh th", vh=2, th=2),
+                )
+            for o in range(2):
+                nc.vector.tensor_copy(
+                    out=g32[:, 8, o, :, :, :],
+                    in_=x32[:, :, 16 + o : 48 + o].rearrange("p u (vh e th) -> p e u vh th", vh=2, th=2)[:, 0, :, :, :],
                 )
 
         def quant_p(t):
             nc.vector.quantize_mx(out=qc[t][:, 0:512].bitcast(FP8X4), scales=qs[t][:, 0:512], in_=grp[t][:, 0:2048])
             nc.vector.quantize_mx(
-                out=qc[t][:, 512:544].bitcast(FP8X4), scales=qs[t][:, 512:544], in_=grp[t][:, 2048:2176]
+                out=qc[t][:, 512:576].bitcast(FP8X4), scales=qs[t][:, 512:576], in_=grp[t][:, 2048:2304]
             )
-            nc.vector.tensor_copy(out=qs2[t][:].bitcast(I32), in_=qs[t][:, 32:544].bitcast(I32))
 
         def regroup(eng_copy, dst, src):
             eng_copy(
@@ -103,41 +102,43 @@ def tile_mlpconv2d_pa_kernel(tc, x, w1, b1, w2, b2, out):
                 in_=src.rearrange("p t (c i) -> p c t i", i=4),
             )
 
-        def regroup_w1(j):
-            cols = slice(256 * j, 256 * j + 256)
-            regroup(nc.vector.tensor_copy, w1g[:, j, 0, :, :], w1r[:, 0:4, cols])
-            regroup(nc.scalar.copy, w1g[:, j, 1, :, :], w1r[:, 4:8, cols])
+        def regroup_w1(jh, j):
+            f0 = 256 * j
+            regroup(nc.vector.tensor_copy, w1g[:, jh, f0 : f0 + P, :], w1r[jh][:, :, f0 : f0 + P])
+            regroup(nc.scalar.copy, w1g[:, jh, f0 + P : f0 + 256, :], w1r[jh][:, :, f0 + P : f0 + 256])
 
-        def quant_w1(j):
+        def quant_w1(jh, j):
+            f0 = 256 * j
             nc.vector.quantize_mx(
-                out=w1c[:, j, :, :].rearrange("p h f -> p (h f)").bitcast(FP8X4),
-                scales=w1s[:, j, :, :].rearrange("p h f -> p (h f)"),
-                in_=w1g[:, j, :, :, :].rearrange("p h f t -> p (h f t)"),
+                out=w1c[:, jh, f0 : f0 + 256].bitcast(FP8X4),
+                scales=w1s[:, jh, f0 : f0 + 256],
+                in_=w1g[:, jh, f0 : f0 + 256, :].rearrange("p f t -> p (f t)"),
             )
 
         banks = {}
 
-        def l1(u):
+        def l1_pass(u, jh):
             t, ft = divmod(u, 8)
-            bank = psum.tile([P, 512], F32, name="l1_%d" % u, tag="bank")
-            banks[u] = bank
-            j, c0 = ft // 2, P * (ft % 2)
+            nc.tensor.matmul_mx(
+                out=banks[u][:],
+                lhsT=w1c[:, jh, P * ft : P * ft + P].bitcast(FP8X4),
+                lhsT_scale=w1s[:, jh, P * ft : P * ft + P],
+                rhs=qc[t][:, 64 * jh : 64 * jh + 512].bitcast(FP8X4),
+                rhs_scale=qs[t][:, 64 * jh : 64 * jh + 512],
+                start=(jh == 0),
+                stop=(jh == 1),
+            )
+
+        def l1(u):
+            banks[u] = psum.tile([P, 512], F32, name="l1_%d" % u, tag="bank")
             for jh in range(2):
-                nc.tensor.matmul_mx(
-                    out=bank[:],
-                    lhsT=w1c[:, j, jh, c0 : c0 + P].bitcast(FP8X4),
-                    lhsT_scale=w1s[:, j, jh, c0 : c0 + P],
-                    rhs=qc[t][:, 32 * jh : 32 * jh + 512].bitcast(FP8X4),
-                    rhs_scale=qs[t][:, 0:512] if jh == 0 else qs2[t][:, 0:512],
-                    start=(jh == 0),
-                    stop=(jh == 1),
-                )
+                l1_pass(u, jh)
 
         def evac(u):
             t, ft = divmod(u, 8)
             nc.scalar.activation(
-                out=hpl[t][:, ft, :].rearrange("p (u a b) -> p u a b", a=16, b=2),
-                in_=banks[u][:].rearrange("p (a b u) -> p u a b", a=16, b=2),
+                out=hpl[t][:, ft, :],
+                in_=banks[u][:],
                 func=RELU,
                 bias=b1f[:, ft : ft + 1],
                 scale=1.0,
@@ -183,32 +184,53 @@ def tile_mlpconv2d_pa_kernel(tc, x, w1, b1, w2, b2, out):
             n, uh = t // 2, t % 2
             r = res[t][:, 2 * k : 2 * k + 2, :]
             nc.scalar.activation(out=r, in_=r, func=RELU)
-            r0 = 512 * uh + 256 * k
-            nc.sync.dma_start(out=out[n, r0 : r0 + 256, :].rearrange("(s p) f -> p s f", p=P), in_=r)
+            if k == 1:
+                rows = out[n].rearrange("(uh s vl q) f -> uh q s vl f", uh=2, s=32, vl=4, q=4)
+                for q in range(4):
+                    nc.sync.dma_start(out=rows[uh, q], in_=res[t][32 * q : 32 * q + 32, :, :])
 
         LEAD = 6
 
+        def step(u):
+            evac(u)
+            if 8 <= u + LEAD < 32:
+                l1(u + LEAD)
+
+        copy_p(0)
+        quant_p(0)
+        for u in range(8):
+            banks[u] = psum.tile([P, 512], F32, name="l1_%d" % u, tag="bank")
+        regroup_w1(0, 0)
+        for j in range(4):
+            if j < 3:
+                regroup_w1(0, j + 1)
+            quant_w1(0, j)
+            l1_pass(2 * j, 0)
+            l1_pass(2 * j + 1, 0)
+        xr1 = keep.tile([P, 32 * PITCH], BF16, name="xr1", tag="raw0", align_bytes=64)
+        xr.append(xr1)
+        for i in range(8):
+            load_x(nc.sync, xr1, 1, 0, 32, i)
+        nc.vector.transpose(out=b1t[:], in_=b1r[:])
+        nc.vector.tensor_copy(out=b1f[:], in_=b1t[:].rearrange("p (ft c) -> p ft c", c=32)[:, :, 0])
+        regroup_w1(1, 0)
+        for j in range(4):
+            if j < 3:
+                regroup_w1(1, j + 1)
+            if j == 0:
+                copy_p(1)
+            if j == 1:
+                quant_p(1)
+            if j == 3:
+                regroup_h(0, 0)
+            quant_w1(1, j)
+            l1_pass(2 * j, 1)
+            l1_pass(2 * j + 1, 1)
+            step(2 * j)
+            step(2 * j + 1)
         b2ps = psum.tile([P, 512], F32, name="b2ps", tag="bank")
         nc.tensor.matmul(out=b2ps[:, 0:256], lhsT=ones[:], rhs=b2z[:], start=True, stop=True)
-        copy_p(0)
-        regroup_w1(0)
-        quant_p(0)
-        nc.vector.transpose(out=b1t[:], in_=b1r[:])
-        nc.vector.tensor_copy(out=b1f[:], in_=b1t[:, 0:8])
-        for j in range(4):
-            quant_w1(j)
-            l1(2 * j)
-            l1(2 * j + 1)
-            if j < 3:
-                regroup_w1(j + 1)
-            evac(2 * j)
-            evac(2 * j + 1)
-            if j == 0:
-                nc.vector.tensor_copy(out=b2bc[:], in_=b2ps[:, 0:256])
-            if j == 2:
-                copy_p(1)
-                regroup_h(0, 0)
-        quant_p(1)
+        nc.vector.tensor_copy(out=b2bc[:], in_=b2ps[:, 0:256])
         for g in range(2):
             regroup(nc.vector.tensor_copy, w2g[:, g, :, :], w2r[:, 4 * g : 4 * g + 4, :])
         quant_h(0, 0)
@@ -217,35 +239,31 @@ def tile_mlpconv2d_pa_kernel(tc, x, w1, b1, w2, b2, out):
             scales=w2s[:].rearrange("p g n -> p (g n)"),
             in_=w2g[:].rearrange("p g n t -> p (g n t)"),
         )
-        for u in range(8, 8 + LEAD):
-            l1(u)
 
         for t in range(1, 5):
-            def step(ft):
+            def tstep(ft):
                 if t < 4:
-                    evac(8 * t + ft)
-                    if 8 * t + ft + LEAD < 32:
-                        l1(8 * t + ft + LEAD)
+                    step(8 * t + ft)
 
-            step(0)
+            tstep(0)
             regroup_h(t - 1, 1)
             if t + 1 < 4:
                 copy_p(t + 1)
-            step(1)
+            tstep(1)
             quant_h(t - 1, 1)
             l2(t - 1, 0)
             l2(t - 1, 1)
             if t + 1 < 4:
                 quant_p(t + 1)
-            step(2)
+            tstep(2)
             add_b2(t - 1, 0)
-            step(3)
+            tstep(3)
             if t < 4:
                 regroup_h(t, 0)
             add_b2(t - 1, 1)
             if t < 4:
                 quant_h(t, 0)
             for ft in range(4, 8):
-                step(ft)
+                tstep(ft)
             relu_store(t - 1, 0)
             relu_store(t - 1, 1)

@@ -10,10 +10,14 @@ I32 = mybir.dt.int32
 FP8X4 = mybir.dt.float8_e4m3fn_x4
 RELU = mybir.ActivationFunctionType.Relu
 ADD = mybir.AluOpType.add
+MAX = mybir.AluOpType.max
 
 FLOPS = 2 * 2048 * 1024 * 1024 + 2 * 2048 * 1024 * 256
 
 P = 128
+ACT_PAIRS = (0, 1)
+W2_SLOT = 8
+R_AGE = 7
 PITCH = 112
 
 
@@ -23,15 +27,14 @@ def tile_mlpconv2d_pa_kernel(tc, x, w1, b1, w2, b2, out):
         keep = ctx.enter_context(tc.tile_pool(name="keep", bufs=1))
         psum = ctx.enter_context(tc.psum_pool(name="psum", bufs=8))
 
-        xr0 = keep.tile([P, 32 * PITCH], BF16, name="xr0", align_bytes=64)
-        xr = [xr0]
+        xr = [keep.tile([P, 32 * PITCH], BF16, name="xr%d" % n, align_bytes=64) for n in range(2)]
         grp = [keep.tile([P, 2304], BF16, name="grp%d" % t, align_bytes=64) for t in range(4)]
         qc = [keep.tile([P, 576], U32, name="qc%d" % t, align_bytes=64) for t in range(4)]
         qs = [keep.tile([P, 576], U8, name="qs%d" % t, align_bytes=64) for t in range(4)]
-        w1r = [keep.tile([P, 4, 1024], BF16, name="w1r%d" % jh, tag="raw%d" % jh, align_bytes=64) for jh in range(2)]
-        w1g = keep.tile([P, 2, 1024, 4], BF16, name="w1g", align_bytes=64)
-        w1c = keep.tile([P, 2, 1024], U32, name="w1c", align_bytes=64)
-        w1s = keep.tile([P, 2, 1024], U8, name="w1s", align_bytes=64)
+        w1r = keep.tile([P, 8, 1024], BF16, name="w1r", align_bytes=64)
+        w1g = keep.tile([P, 4, 2, 256, 4], BF16, name="w1g", align_bytes=64)
+        w1c = keep.tile([P, 4, 2, 256], U32, name="w1c", align_bytes=64)
+        w1s = keep.tile([P, 4, 2, 256], U8, name="w1s", align_bytes=64)
         w2r = keep.tile([P, 8, 256], BF16, name="w2r", align_bytes=64)
         w2g = keep.tile([P, 2, 256, 4], BF16, name="w2g", align_bytes=64)
         w2c = keep.tile([P, 2, 256], U32, name="w2c", align_bytes=64)
@@ -50,30 +53,37 @@ def tile_mlpconv2d_pa_kernel(tc, x, w1, b1, w2, b2, out):
 
         xv = x.rearrange("n c (hh two) w -> n c hh two w", two=2)
 
-        def load_x(eng, tile_, n, u0, nu, i):
-            dst = tile_[:].rearrange("p (u w) -> p u w", w=PITCH)
+        def load_x(eng, n, u0, nu, i):
+            dst = xr[n][:].rearrange("p (u w) -> p u w", w=PITCH)
             eng.dma_start(
                 out=dst[i:P:8, u0 : u0 + nu, 0:70],
                 in_=xv[n, :, u0 + i // 2 : u0 + i // 2 + nu, i % 2, :],
             )
 
+        def load_w1(j):
+            cols = slice(256 * j, 256 * j + 256)
+            nc.sync.dma_start(out=w1r[:, :, cols], in_=w1.rearrange("(p r) f -> p r f", r=8)[:, :, cols])
+
         ctx.enter_context(tc.manual_schedule())
         nc.vector.memset(b1r[:], 0.0)
         nc.vector.memset(b2z[:], 0.0)
         nc.vector.memset(ones[:], 1.0)
-        w1v = w1.rearrange("(p jh t) f -> p jh t f", jh=2, t=4)
-        nc.gpsimd.dma_start(
+        for i in range(7):
+            load_x(nc.scalar if i < 4 else nc.sync, 0, 0, 16, i)
+        load_w1(0)
+        load_x(nc.scalar, 0, 0, 16, 7)
+        load_w1(1)
+        nc.scalar.dma_start(
             out=b1r[0:P:32, :].rearrange("q (ft c) -> q ft c", c=32), in_=b1.rearrange("(ft q c) -> q ft c", q=4, c=32)
         )
-        nc.gpsimd.dma_start(out=b2z[0:1, :], in_=b2.rearrange("(o n) -> o n", o=1))
-        for i in range(7):
-            load_x(nc.scalar if i < 4 else nc.sync, xr0, 0, 0, 16, i)
-        nc.sync.dma_start(out=w1r[0][:], in_=w1v[:, 0, :, :])
-        load_x(nc.sync, xr0, 0, 0, 16, 7)
-        nc.sync.dma_start(out=w1r[1][:], in_=w1v[:, 1, :, :])
+        nc.scalar.dma_start(out=b2z[0:1, :], in_=b2.rearrange("(o n) -> o n", o=1))
         for i in range(8):
-            load_x(nc.sync, xr0, 0, 16, 16, i)
+            load_x(nc.sync, 0, 16, 16, i)
+        load_w1(2)
+        load_w1(3)
         nc.sync.dma_start(out=w2r[:], in_=w2.rearrange("(gt p) n -> p gt n", p=P))
+        for i in range(8):
+            load_x(nc.sync, 1, 0, 32, i)
 
         def copy_p(t):
             n, uh = t // 2, t % 2
@@ -102,40 +112,39 @@ def tile_mlpconv2d_pa_kernel(tc, x, w1, b1, w2, b2, out):
                 in_=src.rearrange("p t (c i) -> p c t i", i=4),
             )
 
-        def regroup_w1(jh, j):
-            f0 = 256 * j
-            regroup(nc.vector.tensor_copy, w1g[:, jh, f0 : f0 + P, :], w1r[jh][:, :, f0 : f0 + P])
-            regroup(nc.scalar.copy, w1g[:, jh, f0 + P : f0 + 256, :], w1r[jh][:, :, f0 + P : f0 + 256])
+        def regroup_w1(j):
+            cols = slice(256 * j, 256 * j + 256)
+            regroup(nc.vector.tensor_copy, w1g[:, j, 0, :, :], w1r[:, 0:4, cols])
+            regroup(nc.scalar.copy if j in ACT_PAIRS else nc.vector.tensor_copy, w1g[:, j, 1, :, :], w1r[:, 4:8, cols])
 
-        def quant_w1(jh, j):
-            f0 = 256 * j
+        def quant_w1(j):
             nc.vector.quantize_mx(
-                out=w1c[:, jh, f0 : f0 + 256].bitcast(FP8X4),
-                scales=w1s[:, jh, f0 : f0 + 256],
-                in_=w1g[:, jh, f0 : f0 + 256, :].rearrange("p f t -> p (f t)"),
+                out=w1c[:, j, :, :].rearrange("p h f -> p (h f)").bitcast(FP8X4),
+                scales=w1s[:, j, :, :].rearrange("p h f -> p (h f)"),
+                in_=w1g[:, j, :, :, :].rearrange("p h f t -> p (h f t)"),
             )
 
+        units = [(t, 4 * g + k) for g in range(2) for t in range(2) for k in range(4)]
+        units += [(t, ft) for t in (2, 3) for ft in range(8)]
         banks = {}
 
-        def l1_pass(u, jh):
-            t, ft = divmod(u, 8)
-            nc.tensor.matmul_mx(
-                out=banks[u][:],
-                lhsT=w1c[:, jh, P * ft : P * ft + P].bitcast(FP8X4),
-                lhsT_scale=w1s[:, jh, P * ft : P * ft + P],
-                rhs=qc[t][:, 64 * jh : 64 * jh + 512].bitcast(FP8X4),
-                rhs_scale=qs[t][:, 64 * jh : 64 * jh + 512],
-                start=(jh == 0),
-                stop=(jh == 1),
-            )
-
         def l1(u):
+            t, ft = units[u]
             banks[u] = psum.tile([P, 512], F32, name="l1_%d" % u, tag="bank")
+            j, c0 = ft // 2, P * (ft % 2)
             for jh in range(2):
-                l1_pass(u, jh)
+                nc.tensor.matmul_mx(
+                    out=banks[u][:],
+                    lhsT=w1c[:, j, jh, c0 : c0 + P].bitcast(FP8X4),
+                    lhsT_scale=w1s[:, j, jh, c0 : c0 + P],
+                    rhs=qc[t][:, 64 * jh : 64 * jh + 512].bitcast(FP8X4),
+                    rhs_scale=qs[t][:, 64 * jh : 64 * jh + 512],
+                    start=(jh == 0),
+                    stop=(jh == 1),
+                )
 
         def evac(u):
-            t, ft = divmod(u, 8)
+            t, ft = units[u]
             nc.scalar.activation(
                 out=hpl[t][:, ft, :],
                 in_=banks[u][:],
@@ -144,14 +153,14 @@ def tile_mlpconv2d_pa_kernel(tc, x, w1, b1, w2, b2, out):
                 scale=1.0,
             )
 
-        def regroup_h(t, g):
-            regroup(nc.vector.tensor_copy, hgr[t][:, g, :, :], hpl[t][:, 4 * g : 4 * g + 4, :])
+        def regroup_h(t, g, c0=0, c1=512, eng_copy=None):
+            regroup(eng_copy or nc.vector.tensor_copy, hgr[t][:, g, c0:c1, :], hpl[t][:, 4 * g : 4 * g + 4, c0:c1])
 
-        def quant_h(t, g):
+        def quant_h(t, g, c0=0, c1=512):
             nc.vector.quantize_mx(
-                out=hc[t][:, g, :].bitcast(FP8X4),
-                scales=hs[t][:, g, :],
-                in_=hgr[t][:, g, :, :].rearrange("p c t -> p (c t)"),
+                out=hc[t][:, g, c0:c1].bitcast(FP8X4),
+                scales=hs[t][:, g, c0:c1],
+                in_=hgr[t][:, g, c0:c1, :].rearrange("p c t -> p (c t)"),
             )
 
         accs = {}
@@ -180,90 +189,83 @@ def tile_mlpconv2d_pa_kernel(tc, x, w1, b1, w2, b2, out):
                 op=ADD,
             )
 
-        def relu_store(t, k):
+        def relu_store(t, k, on_vector=False, halves=False):
             n, uh = t // 2, t % 2
             r = res[t][:, 2 * k : 2 * k + 2, :]
-            nc.scalar.activation(out=r, in_=r, func=RELU)
-            if k == 1:
-                rows = out[n].rearrange("(uh s vl q) f -> uh q s vl f", uh=2, s=32, vl=4, q=4)
+            if on_vector:
+                nc.vector.tensor_scalar(out=r, in0=r, scalar1=0.0, scalar2=None, op0=MAX)
+            else:
+                nc.scalar.activation(out=r, in_=r, func=RELU)
+            rows = out[n].rearrange("(uh s vl q) f -> uh q s vl f", uh=2, s=32, vl=4, q=4)
+            if halves or k == 1:
+                v0 = 2 * k if halves else 0
                 for q in range(4):
-                    nc.sync.dma_start(out=rows[uh, q], in_=res[t][32 * q : 32 * q + 32, :, :])
+                    nc.sync.dma_start(out=rows[uh, q, :, v0 : 2 * k + 2, :], in_=res[t][32 * q : 32 * q + 32, v0 : 2 * k + 2, :])
 
         LEAD = 6
 
-        def step(u):
-            evac(u)
-            if 8 <= u + LEAD < 32:
-                l1(u + LEAD)
+        def issue(s):
+            t, ft = units[s]
+            if t == 0 and ft % 2 == 0:
+                regroup_w1(ft // 2)
+            if ft == 0:
+                copy_p(t)
+            if t == 0 and ft % 2 == 0:
+                quant_w1(ft // 2)
+            if ft == 0:
+                quant_p(t)
+            if s == 0:
+                nc.vector.transpose(out=b1t[:], in_=b1r[:])
+                nc.vector.tensor_copy(out=b1f[:], in_=b1t[:].rearrange("p (ft c) -> p ft c", c=32)[:, :, 0])
+            l1(s)
 
-        copy_p(0)
-        quant_p(0)
-        for u in range(8):
-            banks[u] = psum.tile([P, 512], F32, name="l1_%d" % u, tag="bank")
-        regroup_w1(0, 0)
-        for j in range(4):
-            if j < 3:
-                regroup_w1(0, j + 1)
-            quant_w1(0, j)
-            l1_pass(2 * j, 0)
-            l1_pass(2 * j + 1, 0)
-        xr1 = keep.tile([P, 32 * PITCH], BF16, name="xr1", tag="raw0", align_bytes=64)
-        xr.append(xr1)
-        for i in range(8):
-            load_x(nc.sync, xr1, 1, 0, 32, i)
-        nc.vector.transpose(out=b1t[:], in_=b1r[:])
-        nc.vector.tensor_copy(out=b1f[:], in_=b1t[:].rearrange("p (ft c) -> p ft c", c=32)[:, :, 0])
-        regroup_w1(1, 0)
-        for j in range(4):
-            if j < 3:
-                regroup_w1(1, j + 1)
-            if j == 0:
-                copy_p(1)
-            if j == 1:
-                quant_p(1)
-            if j == 3:
-                regroup_h(0, 0)
-            quant_w1(1, j)
-            l1_pass(2 * j, 1)
-            l1_pass(2 * j + 1, 1)
-            step(2 * j)
-            step(2 * j + 1)
+        def half_done(s, age):
+            if 0 <= s - age < 31 and units[s - age][1] % 4 == 3:
+                return units[s - age][0], units[s - age][1] // 4
+            return None, None
+
+        for s in range(LEAD):
+            issue(s)
         b2ps = psum.tile([P, 512], F32, name="b2ps", tag="bank")
         nc.tensor.matmul(out=b2ps[:, 0:256], lhsT=ones[:], rhs=b2z[:], start=True, stop=True)
-        nc.vector.tensor_copy(out=b2bc[:], in_=b2ps[:, 0:256])
-        for g in range(2):
-            regroup(nc.vector.tensor_copy, w2g[:, g, :, :], w2r[:, 4 * g : 4 * g + 4, :])
-        quant_h(0, 0)
-        nc.vector.quantize_mx(
-            out=w2c[:].rearrange("p g n -> p (g n)").bitcast(FP8X4),
-            scales=w2s[:].rearrange("p g n -> p (g n)"),
-            in_=w2g[:].rearrange("p g n t -> p (g n t)"),
-        )
+        for s in range(32):
+            evac(s)
+            if s == 5:
+                nc.vector.tensor_copy(out=b2bc[:], in_=b2ps[:, 0:256])
+            if s + LEAD < 32:
+                issue(s + LEAD)
+            t, g = half_done(s, 0)
+            if g is not None:
+                regroup_h(t, g)
+            if s == W2_SLOT:
+                for gg in range(2):
+                    regroup(nc.scalar.copy, w2g[:, gg, :, :], w2r[:, 4 * gg : 4 * gg + 4, :])
+            if s == W2_SLOT + 2:
+                nc.vector.quantize_mx(
+                    out=w2c[:].rearrange("p g n -> p (g n)").bitcast(FP8X4),
+                    scales=w2s[:].rearrange("p g n -> p (g n)"),
+                    in_=w2g[:].rearrange("p g n t -> p (g n t)"),
+                )
+            t, g = half_done(s, 1)
+            if g is not None:
+                quant_h(t, g)
+                if g == 1:
+                    l2(t, 0)
+                    l2(t, 1)
+            for k in range(2):
+                t, g = half_done(s, 2 + k)
+                if g == 1:
+                    add_b2(t, k)
+                t, g = half_done(s, R_AGE + k)
+                if g == 1:
+                    relu_store(t, k)
 
-        for t in range(1, 5):
-            def tstep(ft):
-                if t < 4:
-                    step(8 * t + ft)
-
-            tstep(0)
-            regroup_h(t - 1, 1)
-            if t + 1 < 4:
-                copy_p(t + 1)
-            tstep(1)
-            quant_h(t - 1, 1)
-            l2(t - 1, 0)
-            l2(t - 1, 1)
-            if t + 1 < 4:
-                quant_p(t + 1)
-            tstep(2)
-            add_b2(t - 1, 0)
-            tstep(3)
-            if t < 4:
-                regroup_h(t, 0)
-            add_b2(t - 1, 1)
-            if t < 4:
-                quant_h(t, 0)
-            for ft in range(4, 8):
-                tstep(ft)
-            relu_store(t - 1, 0)
-            relu_store(t - 1, 1)
+        regroup_h(3, 1, 0, 256)
+        regroup_h(3, 1, 256, 512, nc.scalar.copy)
+        for k in range(2):
+            quant_h(3, 1, 256 * k, 256 * k + 256)
+            l2(3, k)
+        add_b2(3, 0)
+        relu_store(3, 0, halves=True)
+        add_b2(3, 1)
+        relu_store(3, 1, on_vector=True, halves=True)

@@ -16,7 +16,7 @@ FLOPS = 2 * 2048 * 1024 * 1024 + 2 * 2048 * 1024 * 256
 
 P = 128
 ACT_PAIRS = (0, 1)
-W2_SLOT = 8
+W2_SLOT = 10
 R_AGE = 7
 PITCH = 112
 
@@ -68,22 +68,17 @@ def tile_mlpconv2d_pa_kernel(tc, x, w1, b1, w2, b2, out):
         nc.vector.memset(b1r[:], 0.0)
         nc.vector.memset(b2z[:], 0.0)
         nc.vector.memset(ones[:], 1.0)
-        for i in range(7):
-            load_x(nc.scalar if i < 4 else nc.sync, 0, 0, 16, i)
-        load_w1(0)
-        load_x(nc.scalar, 0, 0, 16, 7)
-        load_w1(1)
-        nc.scalar.dma_start(
+        nc.gpsimd.dma_start(
             out=b1r[0:P:32, :].rearrange("q (ft c) -> q ft c", c=32), in_=b1.rearrange("(ft q c) -> q ft c", q=4, c=32)
         )
-        nc.scalar.dma_start(out=b2z[0:1, :], in_=b2.rearrange("(o n) -> o n", o=1))
+        nc.gpsimd.dma_start(out=b2z[0:1, :], in_=b2.rearrange("(o n) -> o n", o=1))
         for i in range(8):
-            load_x(nc.sync, 0, 16, 16, i)
-        load_w1(2)
-        load_w1(3)
-        nc.sync.dma_start(out=w2r[:], in_=w2.rearrange("(gt p) n -> p gt n", p=P))
+            load_x(nc.scalar if i < 4 else nc.sync, 0, 0, 32, i)
+        for j in range(4):
+            load_w1(j)
         for i in range(8):
             load_x(nc.sync, 1, 0, 32, i)
+        nc.sync.dma_start(out=w2r[:], in_=w2.rearrange("(gt p) n -> p gt n", p=P))
 
         def copy_p(t):
             n, uh = t // 2, t % 2
@@ -206,14 +201,14 @@ def tile_mlpconv2d_pa_kernel(tc, x, w1, b1, w2, b2, out):
 
         def issue(s):
             t, ft = units[s]
-            if t == 0 and ft % 2 == 0:
-                regroup_w1(ft // 2)
-            if ft == 0:
+            if ft == 0 and t >= 2:
                 copy_p(t)
             if t == 0 and ft % 2 == 0:
-                quant_w1(ft // 2)
-            if ft == 0:
+                regroup_w1(ft // 2)
+            if ft == 0 and t >= 2:
                 quant_p(t)
+            if t == 0 and ft % 2 == 0:
+                quant_w1(ft // 2)
             if s == 0:
                 nc.vector.transpose(out=b1t[:], in_=b1r[:])
                 nc.vector.tensor_copy(out=b1f[:], in_=b1t[:].rearrange("p (ft c) -> p ft c", c=32)[:, :, 0])
@@ -224,6 +219,10 @@ def tile_mlpconv2d_pa_kernel(tc, x, w1, b1, w2, b2, out):
                 return units[s - age][0], units[s - age][1] // 4
             return None, None
 
+        for t in range(2):
+            copy_p(t)
+        for t in range(2):
+            quant_p(t)
         for s in range(LEAD):
             issue(s)
         b2ps = psum.tile([P, 512], F32, name="b2ps", tag="bank")

@@ -16,7 +16,7 @@ FLOPS = 2 * 2048 * 1024 * 1024 + 2 * 2048 * 1024 * 256
 
 P = 128
 ACT_PAIRS = (0, 1)
-W2_SLOT = 10
+W2_SLOT = 8
 R_AGE = 7
 PITCH = 112
 
@@ -74,11 +74,13 @@ def tile_mlpconv2d_pa_kernel(tc, x, w1, b1, w2, b2, out):
         nc.gpsimd.dma_start(out=b2z[0:1, :], in_=b2.rearrange("(o n) -> o n", o=1))
         for i in range(8):
             load_x(nc.scalar if i < 4 else nc.sync, 0, 0, 32, i)
-        for j in range(4):
+        for j in range(2):
+            load_w1(j)
+        nc.sync.dma_start(out=w2r[:], in_=w2.rearrange("(gt p) n -> p gt n", p=P))
+        for j in range(2, 4):
             load_w1(j)
         for i in range(8):
             load_x(nc.sync, 1, 0, 32, i)
-        nc.sync.dma_start(out=w2r[:], in_=w2.rearrange("(gt p) n -> p gt n", p=P))
 
         def copy_p(t):
             n, uh = t // 2, t % 2
@@ -235,7 +237,8 @@ def tile_mlpconv2d_pa_kernel(tc, x, w1, b1, w2, b2, out):
                 issue(s + LEAD)
             t, g = half_done(s, 0)
             if g is not None:
-                regroup_h(t, g)
+                regroup_h(t, g, 0, 256)
+                regroup_h(t, g, 256, 512)
             if s == W2_SLOT:
                 for gg in range(2):
                     regroup(nc.scalar.copy, w2g[:, gg, :, :], w2r[:, 4 * gg : 4 * gg + 4, :])
@@ -247,7 +250,8 @@ def tile_mlpconv2d_pa_kernel(tc, x, w1, b1, w2, b2, out):
                 )
             t, g = half_done(s, 1)
             if g is not None:
-                quant_h(t, g)
+                quant_h(t, g, 0, 256)
+                quant_h(t, g, 256, 512)
                 if g == 1:
                     l2(t, 0)
                     l2(t, 1)

@@ -74,11 +74,9 @@ def tile_mlpconv2d_pa_kernel(tc, x, w1, b1, w2, b2, out):
         nc.gpsimd.dma_start(out=b2z[0:1, :], in_=b2.rearrange("(o n) -> o n", o=1))
         for i in range(8):
             load_x(nc.scalar if i < 4 else nc.sync, 0, 0, 32, i)
-        for j in range(2):
+        for j in range(4):
             load_w1(j)
         nc.sync.dma_start(out=w2r[:], in_=w2.rearrange("(gt p) n -> p gt n", p=P))
-        for j in range(2, 4):
-            load_w1(j)
         for i in range(8):
             load_x(nc.sync, 1, 0, 32, i)
 
@@ -115,11 +113,12 @@ def tile_mlpconv2d_pa_kernel(tc, x, w1, b1, w2, b2, out):
             regroup(nc.scalar.copy if j in ACT_PAIRS else nc.vector.tensor_copy, w1g[:, j, 1, :, :], w1r[:, 4:8, cols])
 
         def quant_w1(j):
-            nc.vector.quantize_mx(
-                out=w1c[:, j, :, :].rearrange("p h f -> p (h f)").bitcast(FP8X4),
-                scales=w1s[:, j, :, :].rearrange("p h f -> p (h f)"),
-                in_=w1g[:, j, :, :, :].rearrange("p h f t -> p (h f t)"),
-            )
+            for jh in range(2):
+                nc.vector.quantize_mx(
+                    out=w1c[:, j, jh, :].bitcast(FP8X4),
+                    scales=w1s[:, j, jh, :],
+                    in_=w1g[:, j, jh, :, :].rearrange("p f t -> p (f t)"),
+                )
 
         units = [(t, 4 * g + k) for g in range(2) for t in range(2) for k in range(4)]
         units += [(t, ft) for t in (2, 3) for ft in range(8)]
@@ -263,10 +262,12 @@ def tile_mlpconv2d_pa_kernel(tc, x, w1, b1, w2, b2, out):
                 if g == 1:
                     relu_store(t, k)
 
-        regroup_h(3, 1, 0, 256)
-        regroup_h(3, 1, 256, 512, nc.scalar.copy)
+        for c0 in (0, 128):
+            regroup_h(3, 1, c0, c0 + 128)
+            regroup_h(3, 1, c0 + 256, c0 + 384, nc.scalar.copy)
         for k in range(2):
-            quant_h(3, 1, 256 * k, 256 * k + 256)
+            for c0 in (256 * k, 256 * k + 128):
+                quant_h(3, 1, c0, c0 + 128)
             l2(3, k)
         add_b2(3, 0)
         relu_store(3, 0, halves=True)

@@ -142,8 +142,8 @@ def tile_mlpconv2d_pa_kernel(tc, x, w1, b1, w2, b2, out):
         def evac(u):
             t, ft = units[u]
             nc.scalar.activation(
-                out=hpl[t][:, ft, :],
-                in_=banks[u][:],
+                out=hpl[t][:, ft, :].rearrange("p (vl s q) -> p vl s q", vl=4, q=4),
+                in_=banks[u][:].rearrange("p (vl q s) -> p vl s q", vl=4, q=4),
                 func=RELU,
                 bias=b1f[:, ft : ft + 1],
                 scale=1.0,
@@ -196,7 +196,7 @@ def tile_mlpconv2d_pa_kernel(tc, x, w1, b1, w2, b2, out):
             if halves or k == 1:
                 v0 = 2 * k if halves else 0
                 for q in range(4):
-                    nc.sync.dma_start(out=rows[uh, q, :, v0 : 2 * k + 2, :], in_=res[t][32 * q : 32 * q + 32, v0 : 2 * k + 2, :])
+                    nc.sync.dma_start(out=rows[uh, q, :, v0 : 2 * k + 2, :], in_=res[t][q:P:4, v0 : 2 * k + 2, :])
 
         LEAD = 6
 
@@ -208,11 +208,11 @@ def tile_mlpconv2d_pa_kernel(tc, x, w1, b1, w2, b2, out):
                 regroup_w1(ft // 2)
             if ft == 0 and t >= 2:
                 quant_p(t)
-            if t == 0 and ft % 2 == 0:
-                quant_w1(ft // 2)
             if s == 0:
                 nc.vector.transpose(out=b1t[:], in_=b1r[:])
                 nc.vector.tensor_copy(out=b1f[:], in_=b1t[:].rearrange("p (ft c) -> p ft c", c=32)[:, :, 0])
+            if t == 0 and ft % 2 == 0:
+                quant_w1(ft // 2)
             l1(s)
 
         def half_done(s, age):

from contextlib import ExitStack

import concourse.mybir as mybir

F32 = mybir.dt.float32
BF16 = mybir.dt.bfloat16
U32 = mybir.dt.uint32
U8 = mybir.dt.uint8
I32 = mybir.dt.int32
FP8X4 = mybir.dt.float8_e4m3fn_x4
RELU = mybir.ActivationFunctionType.Relu
ADD = mybir.AluOpType.add
MAX = mybir.AluOpType.max

FLOPS = 2 * 2048 * 1024 * 1024 + 2 * 2048 * 1024 * 256

P = 128
ACT_PAIRS = (0, 1)
W2_SLOT = 8
R_AGE = 7
PITCH = 112


def tile_mlpconv2d_pa_kernel(tc, x, w1, b1, w2, b2, out):
    nc = tc.nc
    with ExitStack() as ctx:
        keep = ctx.enter_context(tc.tile_pool(name="keep", bufs=1))
        psum = ctx.enter_context(tc.psum_pool(name="psum", bufs=8))

        xr = [keep.tile([P, 32 * PITCH], BF16, name="xr%d" % n, align_bytes=64) for n in range(2)]
        grp = [keep.tile([P, 2304], BF16, name="grp%d" % t, align_bytes=64) for t in range(4)]
        qc = [keep.tile([P, 576], U32, name="qc%d" % t, align_bytes=64) for t in range(4)]
        qs = [keep.tile([P, 576], U8, name="qs%d" % t, align_bytes=64) for t in range(4)]
        w1r = keep.tile([P, 8, 1024], BF16, name="w1r", align_bytes=64)
        w1g = keep.tile([P, 4, 2, 256, 4], BF16, name="w1g", align_bytes=64)
        w1c = keep.tile([P, 4, 2, 256], U32, name="w1c", align_bytes=64)
        w1s = keep.tile([P, 4, 2, 256], U8, name="w1s", align_bytes=64)
        w2r = keep.tile([P, 8, 256], BF16, name="w2r", align_bytes=64)
        w2g = keep.tile([P, 2, 256, 4], BF16, name="w2g", align_bytes=64)
        w2c = keep.tile([P, 2, 256], U32, name="w2c", align_bytes=64)
        w2s = keep.tile([P, 2, 256], U8, name="w2s", align_bytes=64)
        b1r = keep.tile([P, 256], BF16, name="b1r", align_bytes=64)
        b1t = keep.tile([P, 256], BF16, name="b1t", align_bytes=64)
        b1f = keep.tile([P, 8], F32, name="b1f")
        b2z = keep.tile([P, 256], BF16, name="b2z")
        ones = keep.tile([P, P], BF16, name="ones")
        b2bc = keep.tile([P, 256], F32, name="b2bc")
        hpl = [keep.tile([P, 8, 512], BF16, name="hpl%d" % t, align_bytes=64) for t in range(4)]
        hgr = [keep.tile([P, 2, 512, 4], BF16, name="hgr%d" % t, align_bytes=64) for t in range(4)]
        hc = [keep.tile([P, 2, 512], U32, name="hc%d" % t, align_bytes=64) for t in range(4)]
        hs = [keep.tile([P, 2, 512], U8, name="hs%d" % t, align_bytes=64) for t in range(4)]
        res = [keep.tile([P, 4, 256], F32, name="res%d" % t) for t in range(4)]

        xv = x.rearrange("n c (hh two) w -> n c hh two w", two=2)

        def load_x(eng, n, u0, nu, i):
            dst = xr[n][:].rearrange("p (u w) -> p u w", w=PITCH)
            eng.dma_start(
                out=dst[i:P:8, u0 : u0 + nu, 0:70],
                in_=xv[n, :, u0 + i // 2 : u0 + i // 2 + nu, i % 2, :],
            )

        def load_w1(j):
            cols = slice(256 * j, 256 * j + 256)
            nc.sync.dma_start(out=w1r[:, :, cols], in_=w1.rearrange("(p r) f -> p r f", r=8)[:, :, cols])

        ctx.enter_context(tc.manual_schedule())
        nc.vector.memset(b1r[:], 0.0)
        nc.vector.memset(b2z[:], 0.0)
        nc.vector.memset(ones[:], 1.0)
        nc.gpsimd.dma_start(
            out=b1r[0:P:32, :].rearrange("q (ft c) -> q ft c", c=32), in_=b1.rearrange("(ft q c) -> q ft c", q=4, c=32)
        )
        nc.gpsimd.dma_start(out=b2z[0:1, :], in_=b2.rearrange("(o n) -> o n", o=1))
        for i in range(8):
            load_x(nc.scalar if i < 4 else nc.sync, 0, 0, 32, i)
        for j in range(4):
            load_w1(j)
        nc.sync.dma_start(out=w2r[:], in_=w2.rearrange("(gt p) n -> p gt n", p=P))
        for i in range(8):
            load_x(nc.sync, 1, 0, 32, i)

        def copy_p(t):
            n, uh = t // 2, t % 2
            x32 = xr[n][:].bitcast(F32).rearrange("p (u w) -> p u w", w=PITCH // 2)[:, 16 * uh : 16 * uh + 16, :]
            g32 = grp[t][:].bitcast(F32).rearrange("p (e o u vh th) -> p e o u vh th", e=9, o=2, u=16, vh=2)
            for o in range(2):
                nc.vector.tensor_copy(
                    out=g32[:, 0:8, o, :, :, :],
                    in_=x32[:, :, o : o + 32].rearrange("p u (vh e th) -> p e u vh th", vh=2, th=2),
                )
            for o in range(2):
                nc.vector.tensor_copy(
                    out=g32[:, 8, o, :, :, :],
                    in_=x32[:, :, 16 + o : 48 + o].rearrange("p u (vh e th) -> p e u vh th", vh=2, th=2)[:, 0, :, :, :],
                )

        def quant_p(t):
            nc.vector.quantize_mx(out=qc[t][:, 0:512].bitcast(FP8X4), scales=qs[t][:, 0:512], in_=grp[t][:, 0:2048])
            nc.vector.quantize_mx(
                out=qc[t][:, 512:576].bitcast(FP8X4), scales=qs[t][:, 512:576], in_=grp[t][:, 2048:2304]
            )

        def regroup(eng_copy, dst, src):
            eng_copy(
                out=dst.rearrange("p (c i) t -> p c t i", i=4),
                in_=src.rearrange("p t (c i) -> p c t i", i=4),
            )

        def regroup_w1(j):
            cols = slice(256 * j, 256 * j + 256)
            regroup(nc.vector.tensor_copy, w1g[:, j, 0, :, :], w1r[:, 0:4, cols])
            regroup(nc.scalar.copy if j in ACT_PAIRS else nc.vector.tensor_copy, w1g[:, j, 1, :, :], w1r[:, 4:8, cols])

        def quant_w1(j):
            for jh in range(2):
                nc.vector.quantize_mx(
                    out=w1c[:, j, jh, :].bitcast(FP8X4),
                    scales=w1s[:, j, jh, :],
                    in_=w1g[:, j, jh, :, :].rearrange("p f t -> p (f t)"),
                )

        units = [(t, 4 * g + k) for g in range(2) for t in range(2) for k in range(4)]
        units += [(t, ft) for t in (2, 3) for ft in range(8)]
        banks = {}

        def l1(u):
            t, ft = units[u]
            banks[u] = psum.tile([P, 512], F32, name="l1_%d" % u, tag="bank")
            j, c0 = ft // 2, P * (ft % 2)
            for jh in range(2):
                nc.tensor.matmul_mx(
                    out=banks[u][:],
                    lhsT=w1c[:, j, jh, c0 : c0 + P].bitcast(FP8X4),
                    lhsT_scale=w1s[:, j, jh, c0 : c0 + P],
                    rhs=qc[t][:, 64 * jh : 64 * jh + 512].bitcast(FP8X4),
                    rhs_scale=qs[t][:, 64 * jh : 64 * jh + 512],
                    start=(jh == 0),
                    stop=(jh == 1),
                )

        def evac(u):
            t, ft = units[u]
            nc.scalar.activation(
                out=hpl[t][:, ft, :].rearrange("p (vl s q) -> p vl s q", vl=4, q=4),
                in_=banks[u][:].rearrange("p (vl q s) -> p vl s q", vl=4, q=4),
                func=RELU,
                bias=b1f[:, ft : ft + 1],
                scale=1.0,
            )

        def regroup_h(t, g, c0=0, c1=512, eng_copy=None):
            regroup(eng_copy or nc.vector.tensor_copy, hgr[t][:, g, c0:c1, :], hpl[t][:, 4 * g : 4 * g + 4, c0:c1])

        def quant_h(t, g, c0=0, c1=512):
            nc.vector.quantize_mx(
                out=hc[t][:, g, c0:c1].bitcast(FP8X4),
                scales=hs[t][:, g, c0:c1],
                in_=hgr[t][:, g, c0:c1, :].rearrange("p c t -> p (c t)"),
            )

        accs = {}

        def l2(t, k):
            acc = psum.tile([P, 2, 256], F32, name="acc%d_%d" % (t, k), tag="bank")
            accs[(t, k)] = acc
            for s in range(2):
                c0 = P * (2 * k + s)
                for g in range(2):
                    nc.tensor.matmul_mx(
                        out=acc[:, s, :],
                        lhsT=hc[t][:, g, c0 : c0 + P].bitcast(FP8X4),
                        lhsT_scale=hs[t][:, g, c0 : c0 + P],
                        rhs=w2c[:, g, :].bitcast(FP8X4),
                        rhs_scale=w2s[:, g, :],
                        start=(g == 0),
                        stop=(g == 1),
                    )

        def add_b2(t, k):
            nc.vector.tensor_tensor(
                out=res[t][:, 2 * k : 2 * k + 2, :],
                in0=accs[(t, k)][:],
                in1=b2bc[:].unsqueeze(1).to_broadcast([P, 2, 256]),
                op=ADD,
            )

        def relu_store(t, k, on_vector=False, halves=False):
            n, uh = t // 2, t % 2
            r = res[t][:, 2 * k : 2 * k + 2, :]
            if on_vector:
                nc.vector.tensor_scalar(out=r, in0=r, scalar1=0.0, scalar2=None, op0=MAX)
            else:
                nc.scalar.activation(out=r, in_=r, func=RELU)
            rows = out[n].rearrange("(uh s vl q) f -> uh q s vl f", uh=2, s=32, vl=4, q=4)
            if halves or k == 1:
                v0 = 2 * k if halves else 0
                for q in range(4):
                    nc.sync.dma_start(out=rows[uh, q, :, v0 : 2 * k + 2, :], in_=res[t][q:P:4, v0 : 2 * k + 2, :])

        LEAD = 6

        def issue(s):
            t, ft = units[s]
            if ft == 0 and t >= 2:
                copy_p(t)
            if t == 0 and ft % 2 == 0:
                regroup_w1(ft // 2)
            if ft == 0 and t >= 2:
                quant_p(t)
            if s == 0:
                nc.vector.transpose(out=b1t[:], in_=b1r[:])
                nc.vector.tensor_copy(out=b1f[:], in_=b1t[:].rearrange("p (ft c) -> p ft c", c=32)[:, :, 0])
            if t == 0 and ft % 2 == 0:
                quant_w1(ft // 2)
            l1(s)

        def half_done(s, age):
            if 0 <= s - age < 31 and units[s - age][1] % 4 == 3:
                return units[s - age][0], units[s - age][1] // 4
            return None, None

        for t in range(2):
            copy_p(t)
        for t in range(2):
            quant_p(t)
        for s in range(LEAD):
            issue(s)
        b2ps = psum.tile([P, 512], F32, name="b2ps", tag="bank")
        nc.tensor.matmul(out=b2ps[:, 0:256], lhsT=ones[:], rhs=b2z[:], start=True, stop=True)
        for s in range(32):
            evac(s)
            if s == 5:
                nc.vector.tensor_copy(out=b2bc[:], in_=b2ps[:, 0:256])
            if s + LEAD < 32:
                issue(s + LEAD)
            t, g = half_done(s, 0)
            if g is not None:
                regroup_h(t, g, 0, 256)
                regroup_h(t, g, 256, 512)
            if s == W2_SLOT:
                for gg in range(2):
                    regroup(nc.scalar.copy, w2g[:, gg, :, :], w2r[:, 4 * gg : 4 * gg + 4, :])
            if s == W2_SLOT + 2:
                nc.vector.quantize_mx(
                    out=w2c[:].rearrange("p g n -> p (g n)").bitcast(FP8X4),
                    scales=w2s[:].rearrange("p g n -> p (g n)"),
                    in_=w2g[:].rearrange("p g n t -> p (g n t)"),
                )
            t, g = half_done(s, 1)
            if g is not None:
                quant_h(t, g, 0, 256)
                quant_h(t, g, 256, 512)
                if g == 1:
                    l2(t, 0)
                    l2(t, 1)
            for k in range(2):
                t, g = half_done(s, 2 + k)
                if g == 1:
                    add_b2(t, k)
                t, g = half_done(s, R_AGE + k)
                if g == 1:
                    relu_store(t, k)

        for c0 in (0, 128):
            regroup_h(3, 1, c0, c0 + 128)
            regroup_h(3, 1, c0 + 256, c0 + 384, nc.scalar.copy)
        for k in range(2):
            for c0 in (256 * k, 256 * k + 128):
                quant_h(3, 1, c0, c0 + 128)
            l2(3, k)
        add_b2(3, 0)
        relu_store(3, 0, halves=True)
        add_b2(3, 1)
        relu_store(3, 1, on_vector=True, halves=True)
